import numpy as np
import ml_dtypes


def mxq(x, axis, fmt="e4m3"):
    dtype, down = {"e4m3": (ml_dtypes.float8_e4m3fn, 7), "e5m2": (ml_dtypes.float8_e5m2, 14)}[fmt]
    v = np.moveaxis(np.asarray(x, np.float32).astype(ml_dtypes.bfloat16).astype(np.float64), axis, -1)
    blocks = v.reshape(v.shape[:-1] + (-1, 32))
    amax = np.abs(blocks).max(-1, keepdims=True)
    byte = np.maximum(np.where(amax > 0, np.frexp(amax)[1] - 1 + 127, 0) - down, 1)
    scale = np.exp2(byte - 127.0)
    codes = (blocks / scale).astype(np.float32).astype(dtype).astype(np.float64)
    return np.moveaxis((codes * scale).reshape(v.shape), -1, axis)


WIDE = False


def mx_kscale(k):
    if not WIDE:
        return np.ones(k)
    levels = np.array([20, -20, 10, -10, 0])
    if k % 512:
        return np.exp2(np.random.permutation(np.resize(levels, k // 32))).repeat(32)
    a = np.empty((k // 512, 16))
    for p in range(k // 512):
        a[p, :8] = np.random.permutation(np.resize(levels, 8))
        for g in range(8):
            far = levels[np.abs(levels - a[p, g]) >= 10]
            a[p, g + 8] = far[np.random.randint(len(far))]
    return np.exp2(a.ravel()).repeat(32)


BF16 = ml_dtypes.bfloat16


def bf(x):
    return np.asarray(x, np.float32).astype(BF16)


def f64(x):
    return np.asarray(x).astype(np.float64)


N, LMAX, CIN, COUT = 512, 1, 128, 8192
NL = LMAX + 1
NM = NL * NL


def setup_inputs():
    u = mx_kscale(COUT)
    x = np.random.standard_normal((N, NM, CIN))
    weights = np.random.standard_normal((NL, CIN, COUT)) / np.sqrt(CIN) / u
    path_weights = 1.0 + 0.3 * np.random.standard_normal(NL)
    g = np.random.standard_normal((N, NM, COUT)) * np.exp2(np.random.randint(-12, 1, (N, NM, 1))) * 16.0 * u
    return {"x": bf(x), "weights": bf(weights), "path_weights": bf(path_weights), "grad_out": bf(g)}


def reference(x, weights, path_weights, grad_out):
    weights, path_weights, g = f64(weights), f64(path_weights), f64(grad_out)
    blocks = []
    for l in range(LMAX + 1):
        start = l * l
        end = start + (2 * l + 1)
        blk = mxq(g[:, start:end, :], 2, "e5m2") @ mxq(weights[l], 1, "e4m3").T
        blocks.append(path_weights[l] * blk)
    return np.concatenate(blocks, axis=1)

@@ -1,0 +1,176 @@
+from contextlib import ExitStack
+
+import concourse.mybir as mybir
+from concourse.masks import make_identity
+
+BF16 = mybir.dt.bfloat16
+F32 = mybir.dt.float32
+U32 = mybir.dt.uint32
+U8 = mybir.dt.uint8
+E4M3X4 = mybir.dt.float8_e4m3fn_x4
+E5M2X4 = mybir.dt.float8_e5m2_x4
+
+P = 128
+PACK = 4
+K_PASS = P * PACK
+PAIRS = K_PASS // 2
+
+NODES = 512
+ROWS = 4
+DEGREE_OF_ROW = [0, 1, 1, 1]
+DEGREES = 2
+C_IN = 128
+K = 8192
+PASSES = K // K_PASS
+NODE_TILES = NODES // P
+BLOCKS = 4
+
+CHUNK_PASSES = 4
+CHUNK_K = CHUNK_PASSES * K_PASS
+CHUNKS = PASSES // CHUNK_PASSES
+
+FLOPS = 2 * NODES * ROWS * K * C_IN
+BYTES = 2 * (DEGREES * C_IN * K + NODES * ROWS * K + DEGREES) + 4 * NODES * ROWS * C_IN
+
+
+def tile_linear_pa_k_kernel(tc, x, weights, path_weights, grad_out, out):
+    nc = tc.nc
+    with ExitStack() as ctx:
+        consts = ctx.enter_context(tc.tile_pool(name="consts", bufs=1))
+        w_raw_pool = ctx.enter_context(tc.tile_pool(name="w_raw", bufs=2))
+        g_raw_pool = ctx.enter_context(tc.tile_pool(name="g_raw", bufs=6))
+        grouped_pool = ctx.enter_context(tc.tile_pool(name="grouped", bufs=4))
+        g_mx_pool = ctx.enter_context(tc.tile_pool(name="g_mx", bufs=3))
+        out_pool = ctx.enter_context(tc.tile_pool(name="out", bufs=2))
+        bank_pool = ctx.enter_context(tc.psum_pool(name="bank", bufs=6))
+        acc_pool = ctx.enter_context(tc.psum_pool(name="acc", bufs=2))
+        ctx.enter_context(tc.manual_schedule())
+
+        ident = consts.tile([P, P], F32)
+        make_identity(nc, ident[:])
+
+        pw_bf16 = consts.tile([P, DEGREES], BF16)
+        nc.scalar.dma_start(out=pw_bf16[:], in_=path_weights.partition_broadcast(P))
+        pw = consts.tile([P, DEGREES], F32)
+        nc.vector.tensor_copy(out=pw[:], in_=pw_bf16[:])
+
+        def transpose_blocks(blocks, vector_helps):
+            grouped = grouped_pool.tile([P, BLOCKS * P * PACK], BF16, align_bytes=64)
+            grouped_words = grouped[:].bitcast(F32).rearrange("p (b r u) -> p b r u", b=BLOCKS, u=2)
+            for half in range(2):
+                bank = bank_pool.tile([P, 2, 2, P], F32, tag="bank")
+                for b in range(2):
+                    for u in range(2):
+                        nc.tensor.transpose(
+                            bank[:, b, u, :], blocks[2 * half + b][:, u:PAIRS:2], ident[:]
+                        )
+                dst = grouped_words[:, 2 * half : 2 * half + 2, :, :]
+                src = bank[:].rearrange("p b u r -> p b r u")
+                if half == 1 and vector_helps:
+                    nc.vector.tensor_copy(out=dst, in_=src)
+                else:
+                    nc.scalar.copy(out=dst, in_=src)
+            return grouped
+
+        def transpose_and_quantise(block_lists, codes, scales, fmt):
+            waiting = []
+            for i in range(len(block_lists)):
+                waiting.append(transpose_blocks(block_lists[i], vector_helps=(i % 2 == 1)))
+                if i >= 1:
+                    nc.vector.quantize_mx(
+                        out=codes[i - 1].bitcast(fmt), scales=scales[i - 1], in_=waiting[i - 1][:]
+                    )
+            last = len(block_lists) - 1
+            nc.vector.quantize_mx(out=codes[last].bitcast(fmt), scales=scales[last], in_=waiting[last][:])
+
+        def prepare_weights(degree):
+            w_raw = w_raw_pool.tile([P, K], BF16)
+            nc.sync.dma_start(out=w_raw[:], in_=weights[degree])
+            w_words = w_raw[:].bitcast(F32)
+            w_codes = consts.tile([P, PASSES * C_IN], U32, align_bytes=64, name="w_codes%d" % degree)
+            w_scales = consts.tile([P, PASSES * C_IN], U8, align_bytes=64, name="w_scales%d" % degree)
+            width = BLOCKS * C_IN
+            calls = PASSES // BLOCKS
+            transpose_and_quantise(
+                [
+                    [w_words[:, (BLOCKS * q + i) * PAIRS : (BLOCKS * q + i + 1) * PAIRS] for i in range(BLOCKS)]
+                    for q in range(calls)
+                ],
+                [w_codes[:, q * width : (q + 1) * width] for q in range(calls)],
+                [w_scales[:, q * width : (q + 1) * width] for q in range(calls)],
+                E4M3X4,
+            )
+            return w_codes, w_scales
+
+        def prepare_chunk(row, chunk):
+            g_raw = g_raw_pool.tile([P, NODE_TILES, CHUNK_K], BF16)
+            nc.sync.dma_start(
+                out=g_raw[:],
+                in_=grad_out[:, row, chunk * CHUNK_K : (chunk + 1) * CHUNK_K].rearrange(
+                    "(t p) k -> p t k", p=P
+                ),
+            )
+            g_words = g_raw[:].bitcast(F32)
+            g_codes = g_mx_pool.tile([P, CHUNK_PASSES, NODES], U32, align_bytes=64)
+            g_scales = g_mx_pool.tile([P, CHUNK_PASSES, NODES], U8, align_bytes=64)
+            transpose_and_quantise(
+                [
+                    [g_words[:, t, c * PAIRS : (c + 1) * PAIRS] for t in range(NODE_TILES)]
+                    for c in range(CHUNK_PASSES)
+                ],
+                [g_codes[:, c, :] for c in range(CHUNK_PASSES)],
+                [g_scales[:, c, :] for c in range(CHUNK_PASSES)],
+                E5M2X4,
+            )
+            return g_codes, g_scales
+
+        def multiply(acc, chunk, w_codes, w_scales, g_codes, g_scales):
+            for c in range(CHUNK_PASSES):
+                k_pass = chunk * CHUNK_PASSES + c
+                nc.tensor.matmul_mx(
+                    out=acc[:],
+                    lhsT=w_codes[:, k_pass * C_IN : (k_pass + 1) * C_IN].bitcast(E4M3X4),
+                    lhsT_scale=w_scales[:, k_pass * C_IN : (k_pass + 1) * C_IN],
+                    rhs=g_codes[:, c, :].bitcast(E5M2X4),
+                    rhs_scale=g_scales[:, c, :],
+                    start=(k_pass == 0),
+                    stop=(k_pass == PASSES - 1),
+                )
+
+        def write_out(row, acc):
+            degree = DEGREE_OF_ROW[row]
+            scaled = out_pool.tile([P, NODES], F32)
+            nc.vector.tensor_scalar(
+                out=scaled[:],
+                in0=acc[:],
+                scalar1=pw[:, degree : degree + 1],
+                scalar2=None,
+                op0=mybir.AluOpType.mult,
+            )
+            back = bank_pool.tile([P, NODE_TILES, C_IN], F32, tag="bank")
+            for t in range(NODE_TILES):
+                nc.tensor.transpose(back[:, t, :], scaled[:, t * P : (t + 1) * P], ident[:])
+            result = out_pool.tile([P, NODE_TILES, C_IN], F32)
+            nc.scalar.copy(out=result[:], in_=back[:])
+            nc.scalar.dma_start(out=out[:, row, :].rearrange("(t p) c -> p t c", p=P), in_=result[:])
+
+        steps = [(row, chunk) for row in range(ROWS) for chunk in range(CHUNKS)]
+        w_mx = {}
+        g_mx = {}
+        acc_of_row = {}
+        for i in range(len(steps) + 1):
+            if i < len(steps):
+                row, chunk = steps[i]
+                degree = DEGREE_OF_ROW[row]
+                if degree not in w_mx:
+                    w_mx[degree] = prepare_weights(degree)
+                g_mx[i] = prepare_chunk(row, chunk)
+            if i >= 1:
+                row, chunk = steps[i - 1]
+                if chunk == 0:
+                    acc_of_row[row] = acc_pool.tile([P, NODES], F32, name="acc")
+                w_codes, w_scales = w_mx[DEGREE_OF_ROW[row]]
+                g_codes, g_scales = g_mx[i - 1]
+                multiply(acc_of_row[row], chunk, w_codes, w_scales, g_codes, g_scales)
+                if chunk == CHUNKS - 1:
+                    write_out(row, acc_of_row[row])

@@ -28,6 +28,8 @@ BLOCKS = 4
 CHUNK_PASSES = 4
 CHUNK_K = CHUNK_PASSES * K_PASS
 CHUNKS = PASSES // CHUNK_PASSES
+LOAD_AHEAD = 18
+RUN = 2
 
 FLOPS = 2 * NODES * ROWS * K * C_IN
 BYTES = 2 * (DEGREES * C_IN * K + NODES * ROWS * K + DEGREES) + 4 * NODES * ROWS * C_IN
@@ -37,10 +39,11 @@ def tile_linear_pa_k_kernel(tc, x, weights, path_weights, grad_out, out):
     nc = tc.nc
     with ExitStack() as ctx:
         consts = ctx.enter_context(tc.tile_pool(name="consts", bufs=1))
-        w_raw_pool = ctx.enter_context(tc.tile_pool(name="w_raw", bufs=2))
+        w_raw_pool = ctx.enter_context(tc.tile_pool(name="w_raw", bufs=6))
         g_raw_pool = ctx.enter_context(tc.tile_pool(name="g_raw", bufs=6))
-        grouped_pool = ctx.enter_context(tc.tile_pool(name="grouped", bufs=4))
-        g_mx_pool = ctx.enter_context(tc.tile_pool(name="g_mx", bufs=3))
+        sorted_pool = ctx.enter_context(tc.tile_pool(name="sorted", bufs=4))
+        grouped_pool = ctx.enter_context(tc.tile_pool(name="grouped", bufs=5))
+        g_mx_pool = ctx.enter_context(tc.tile_pool(name="g_mx", bufs=6))
         out_pool = ctx.enter_context(tc.tile_pool(name="out", bufs=2))
         bank_pool = ctx.enter_context(tc.psum_pool(name="bank", bufs=6))
         acc_pool = ctx.enter_context(tc.psum_pool(name="acc", bufs=2))
@@ -54,99 +57,120 @@ def tile_linear_pa_k_kernel(tc, x, weights, path_weights, grad_out, out):
         pw = consts.tile([P, DEGREES], F32)
         nc.vector.tensor_copy(out=pw[:], in_=pw_bf16[:])
 
-        def transpose_blocks(blocks, vector_helps):
-            grouped = grouped_pool.tile([P, BLOCKS * P * PACK], BF16, align_bytes=64)
-            grouped_words = grouped[:].bitcast(F32).rearrange("p (b r u) -> p b r u", b=BLOCKS, u=2)
+        w_codes = []
+        w_scales = []
+        for degree in range(DEGREES):
+            codes = consts.tile([P, PASSES * C_IN], U32, align_bytes=64, name="w_codes%d" % degree)
+            scales = consts.tile([P, PASSES * C_IN], U8, align_bytes=64, name="w_scales%d" % degree)
+            w_codes.append(codes)
+            w_scales.append(scales)
+
+        groups = []
+        for row in range(ROWS):
+            for chunk in range(CHUNKS):
+                if row == 0 or DEGREE_OF_ROW[row] != DEGREE_OF_ROW[row - 1]:
+                    groups.append(("w", DEGREE_OF_ROW[row], chunk))
+                for c in range(CHUNK_PASSES):
+                    groups.append(("g", row, chunk * CHUNK_PASSES + c))
+
+        raw = {}
+        blocks = {}
+        sorted_words = {}
+        grouped = {}
+        g_mx = {}
+        acc_of_row = {}
+
+        def load(i):
+            kind, a, b = groups[i]
+            if kind == "w":
+                w_raw = w_raw_pool.tile([P, CHUNK_K], BF16)
+                nc.sync.dma_start(out=w_raw[:], in_=weights[a][:, b * CHUNK_K : (b + 1) * CHUNK_K])
+                blocks[i] = w_raw[:].bitcast(F32).rearrange("p (b w) -> p b w", b=BLOCKS)
+            else:
+                chunk, c = divmod(b, CHUNK_PASSES)
+                if c == 0:
+                    g_raw = g_raw_pool.tile([P, NODE_TILES, CHUNK_K], BF16)
+                    nc.sync.dma_start(
+                        out=g_raw[:],
+                        in_=grad_out[:, a, chunk * CHUNK_K : (chunk + 1) * CHUNK_K].rearrange(
+                            "(t p) k -> p t k", p=P
+                        ),
+                    )
+                    raw[(a, chunk)] = g_raw
+                blocks[i] = raw[(a, chunk)][:].bitcast(F32)[:, :, c * PAIRS : (c + 1) * PAIRS]
+
+        def is_sorted(i):
+            return i >= 4 and i < len(groups) - 2 and i % 4 != 3
+
+        def sort_words(i):
+            if is_sorted(i):
+                tile = sorted_pool.tile([P, BLOCKS, 2, P], F32)
+                nc.vector.tensor_copy(out=tile[:], in_=blocks[i].rearrange("p b (w u) -> p b u w", u=2))
+                sorted_words[i] = tile
+
+        def transpose(i):
+            grouped[i] = grouped_pool.tile([P, BLOCKS * P * PACK], BF16, align_bytes=64, name="grouped")
+            words = grouped[i][:].bitcast(F32).rearrange("p (b r u) -> p b r u", b=BLOCKS, u=2)
             for half in range(2):
                 bank = bank_pool.tile([P, 2, 2, P], F32, tag="bank")
                 for b in range(2):
                     for u in range(2):
-                        nc.tensor.transpose(
-                            bank[:, b, u, :], blocks[2 * half + b][:, u:PAIRS:2], ident[:]
-                        )
-                dst = grouped_words[:, 2 * half : 2 * half + 2, :, :]
-                src = bank[:].rearrange("p b u r -> p b r u")
-                if half == 1 and vector_helps:
-                    nc.vector.tensor_copy(out=dst, in_=src)
-                else:
-                    nc.scalar.copy(out=dst, in_=src)
-            return grouped
-
-        def transpose_and_quantise(block_lists, codes, scales, fmt):
-            waiting = []
-            for i in range(len(block_lists)):
-                waiting.append(transpose_blocks(block_lists[i], vector_helps=(i % 2 == 1)))
-                if i >= 1:
-                    nc.vector.quantize_mx(
-                        out=codes[i - 1].bitcast(fmt), scales=scales[i - 1], in_=waiting[i - 1][:]
-                    )
-            last = len(block_lists) - 1
-            nc.vector.quantize_mx(out=codes[last].bitcast(fmt), scales=scales[last], in_=waiting[last][:])
-
-        def prepare_weights(degree):
-            w_raw = w_raw_pool.tile([P, K], BF16)
-            nc.sync.dma_start(out=w_raw[:], in_=weights[degree])
-            w_words = w_raw[:].bitcast(F32)
-            w_codes = consts.tile([P, PASSES * C_IN], U32, align_bytes=64, name="w_codes%d" % degree)
-            w_scales = consts.tile([P, PASSES * C_IN], U8, align_bytes=64, name="w_scales%d" % degree)
-            width = BLOCKS * C_IN
-            calls = PASSES // BLOCKS
-            transpose_and_quantise(
-                [
-                    [w_words[:, (BLOCKS * q + i) * PAIRS : (BLOCKS * q + i + 1) * PAIRS] for i in range(BLOCKS)]
-                    for q in range(calls)
-                ],
-                [w_codes[:, q * width : (q + 1) * width] for q in range(calls)],
-                [w_scales[:, q * width : (q + 1) * width] for q in range(calls)],
-                E4M3X4,
-            )
-            return w_codes, w_scales
-
-        def prepare_chunk(row, chunk):
-            g_raw = g_raw_pool.tile([P, NODE_TILES, CHUNK_K], BF16)
-            nc.sync.dma_start(
-                out=g_raw[:],
-                in_=grad_out[:, row, chunk * CHUNK_K : (chunk + 1) * CHUNK_K].rearrange(
-                    "(t p) k -> p t k", p=P
-                ),
-            )
-            g_words = g_raw[:].bitcast(F32)
-            g_codes = g_mx_pool.tile([P, CHUNK_PASSES, NODES], U32, align_bytes=64)
-            g_scales = g_mx_pool.tile([P, CHUNK_PASSES, NODES], U8, align_bytes=64)
-            transpose_and_quantise(
-                [
-                    [g_words[:, t, c * PAIRS : (c + 1) * PAIRS] for t in range(NODE_TILES)]
-                    for c in range(CHUNK_PASSES)
-                ],
-                [g_codes[:, c, :] for c in range(CHUNK_PASSES)],
-                [g_scales[:, c, :] for c in range(CHUNK_PASSES)],
-                E5M2X4,
-            )
-            return g_codes, g_scales
-
-        def multiply(acc, chunk, w_codes, w_scales, g_codes, g_scales):
-            for c in range(CHUNK_PASSES):
-                k_pass = chunk * CHUNK_PASSES + c
-                nc.tensor.matmul_mx(
-                    out=acc[:],
-                    lhsT=w_codes[:, k_pass * C_IN : (k_pass + 1) * C_IN].bitcast(E4M3X4),
-                    lhsT_scale=w_scales[:, k_pass * C_IN : (k_pass + 1) * C_IN],
-                    rhs=g_codes[:, c, :].bitcast(E5M2X4),
-                    rhs_scale=g_scales[:, c, :],
-                    start=(k_pass == 0),
-                    stop=(k_pass == PASSES - 1),
+                        block = 2 * half + b
+                        if is_sorted(i):
+                            in_ = sorted_words[i][:, block, u, :]
+                        else:
+                            in_ = blocks[i][:, block, u:PAIRS:2]
+                        nc.tensor.transpose(bank[:, b, u, :], in_, ident[:])
+                nc.scalar.copy(
+                    out=words[:, 2 * half : 2 * half + 2, :, :], in_=bank[:].rearrange("p b u r -> p b r u")
                 )
 
-        def write_out(row, acc):
+        def quantise(i):
+            kind, a, b = groups[i]
+            if kind == "w":
+                width = BLOCKS * C_IN
+                cols = slice(b * width, (b + 1) * width)
+                nc.vector.quantize_mx(
+                    out=w_codes[a][:, cols].bitcast(E4M3X4), scales=w_scales[a][:, cols], in_=grouped[i][:]
+                )
+            else:
+                codes = g_mx_pool.tile([P, NODES], U32, align_bytes=64)
+                scales = g_mx_pool.tile([P, NODES], U8, align_bytes=64)
+                nc.vector.quantize_mx(out=codes[:].bitcast(E5M2X4), scales=scales[:], in_=grouped[i][:])
+                g_mx[i] = (codes, scales)
+
+        def multiply(i):
+            kind, row, k_pass = groups[i]
+            if kind == "w":
+                return
+            if k_pass == 0:
+                acc_of_row[row] = acc_pool.tile([P, NODES], F32, name="acc")
+            degree = DEGREE_OF_ROW[row]
+            cols = slice(k_pass * C_IN, (k_pass + 1) * C_IN)
+            codes, scales = g_mx[i]
+            nc.tensor.matmul_mx(
+                out=acc_of_row[row][:],
+                lhsT=w_codes[degree][:, cols].bitcast(E4M3X4),
+                lhsT_scale=w_scales[degree][:, cols],
+                rhs=codes[:].bitcast(E5M2X4),
+                rhs_scale=scales[:],
+                start=(k_pass == 0),
+                stop=(k_pass == PASSES - 1),
+            )
+
+        def scale_row(row):
             degree = DEGREE_OF_ROW[row]
             scaled = out_pool.tile([P, NODES], F32)
             nc.vector.tensor_scalar(
                 out=scaled[:],
-                in0=acc[:],
+                in0=acc_of_row[row][:],
                 scalar1=pw[:, degree : degree + 1],
                 scalar2=None,
                 op0=mybir.AluOpType.mult,
             )
+            return scaled
+
+        def write_out(row, scaled):
             back = bank_pool.tile([P, NODE_TILES, C_IN], F32, tag="bank")
             for t in range(NODE_TILES):
                 nc.tensor.transpose(back[:, t, :], scaled[:, t * P : (t + 1) * P], ident[:])
@@ -154,23 +178,30 @@ def tile_linear_pa_k_kernel(tc, x, weights, path_weights, grad_out, out):
             nc.scalar.copy(out=result[:], in_=back[:])
             nc.scalar.dma_start(out=out[:, row, :].rearrange("(t p) c -> p t c", p=P), in_=result[:])
 
-        steps = [(row, chunk) for row in range(ROWS) for chunk in range(CHUNKS)]
-        w_mx = {}
-        g_mx = {}
-        acc_of_row = {}
-        for i in range(len(steps) + 1):
-            if i < len(steps):
-                row, chunk = steps[i]
-                degree = DEGREE_OF_ROW[row]
-                if degree not in w_mx:
-                    w_mx[degree] = prepare_weights(degree)
-                g_mx[i] = prepare_chunk(row, chunk)
-            if i >= 1:
-                row, chunk = steps[i - 1]
-                if chunk == 0:
-                    acc_of_row[row] = acc_pool.tile([P, NODES], F32, name="acc")
-                w_codes, w_scales = w_mx[DEGREE_OF_ROW[row]]
-                g_codes, g_scales = g_mx[i - 1]
-                multiply(acc_of_row[row], chunk, w_codes, w_scales, g_codes, g_scales)
-                if chunk == CHUNKS - 1:
-                    write_out(row, acc_of_row[row])
+        runs = [list(range(i, min(i + RUN, len(groups)))) for i in range(0, len(groups), RUN)]
+        loaded = 0
+        finished = []
+        for s in range(len(runs) + 2):
+            while loaded < min(RUN * s + LOAD_AHEAD, len(groups)):
+                load(loaded)
+                loaded += 1
+            if s + 1 < len(runs):
+                for i in runs[s + 1]:
+                    sort_words(i)
+            for row, scaled in finished:
+                write_out(row, scaled)
+            finished = []
+            if s < len(runs):
+                for i in runs[s]:
+                    transpose(i)
+            if 1 <= s <= len(runs):
+                for i in runs[s - 1]:
+                    quantise(i)
+            if s >= 2:
+                for i in runs[s - 2]:
+                    multiply(i)
+                    kind, row, k_pass = groups[i]
+                    if kind == "g" and k_pass == PASSES - 1:
+                        finished.append((row, scale_row(row)))
+        for row, scaled in finished:
+            write_out(row, scaled)

@@ -25,9 +25,10 @@ PASSES = K // K_PASS
 NODE_TILES = NODES // P
 BLOCKS = 4
 
-CHUNK_PASSES = 4
-CHUNK_K = CHUNK_PASSES * K_PASS
-CHUNKS = PASSES // CHUNK_PASSES
+W_PASSES = 4
+W_CHUNK = W_PASSES * K_PASS
+G_PASSES = 2
+G_CHUNK = G_PASSES * K_PASS
 LOAD_AHEAD = 18
 RUN = 2
 
@@ -40,7 +41,7 @@ def tile_linear_pa_k_kernel(tc, x, weights, path_weights, grad_out, out):
     with ExitStack() as ctx:
         consts = ctx.enter_context(tc.tile_pool(name="consts", bufs=1))
         w_raw_pool = ctx.enter_context(tc.tile_pool(name="w_raw", bufs=6))
-        g_raw_pool = ctx.enter_context(tc.tile_pool(name="g_raw", bufs=6))
+        g_raw_pool = ctx.enter_context(tc.tile_pool(name="g_raw", bufs=12))
         sorted_pool = ctx.enter_context(tc.tile_pool(name="sorted", bufs=4))
         grouped_pool = ctx.enter_context(tc.tile_pool(name="grouped", bufs=5))
         g_mx_pool = ctx.enter_context(tc.tile_pool(name="g_mx", bufs=6))
@@ -67,11 +68,11 @@ def tile_linear_pa_k_kernel(tc, x, weights, path_weights, grad_out, out):
 
         groups = []
         for row in range(ROWS):
-            for chunk in range(CHUNKS):
-                if row == 0 or DEGREE_OF_ROW[row] != DEGREE_OF_ROW[row - 1]:
-                    groups.append(("w", DEGREE_OF_ROW[row], chunk))
-                for c in range(CHUNK_PASSES):
-                    groups.append(("g", row, chunk * CHUNK_PASSES + c))
+            first_of_degree = row == 0 or DEGREE_OF_ROW[row] != DEGREE_OF_ROW[row - 1]
+            for k_pass in range(PASSES):
+                if first_of_degree and k_pass % W_PASSES == 0:
+                    groups.append(("w", DEGREE_OF_ROW[row], k_pass // W_PASSES))
+                groups.append(("g", row, k_pass))
 
         raw = {}
         blocks = {}
@@ -83,16 +84,16 @@ def tile_linear_pa_k_kernel(tc, x, weights, path_weights, grad_out, out):
         def load(i):
             kind, a, b = groups[i]
             if kind == "w":
-                w_raw = w_raw_pool.tile([P, CHUNK_K], BF16)
-                nc.sync.dma_start(out=w_raw[:], in_=weights[a][:, b * CHUNK_K : (b + 1) * CHUNK_K])
+                w_raw = w_raw_pool.tile([P, W_CHUNK], BF16)
+                nc.sync.dma_start(out=w_raw[:], in_=weights[a][:, b * W_CHUNK : (b + 1) * W_CHUNK])
                 blocks[i] = w_raw[:].bitcast(F32).rearrange("p (b w) -> p b w", b=BLOCKS)
             else:
-                chunk, c = divmod(b, CHUNK_PASSES)
+                chunk, c = divmod(b, G_PASSES)
                 if c == 0:
-                    g_raw = g_raw_pool.tile([P, NODE_TILES, CHUNK_K], BF16)
+                    g_raw = g_raw_pool.tile([P, NODE_TILES, G_CHUNK], BF16)
                     nc.sync.dma_start(
                         out=g_raw[:],
-                        in_=grad_out[:, a, chunk * CHUNK_K : (chunk + 1) * CHUNK_K].rearrange(
+                        in_=grad_out[:, a, chunk * G_CHUNK : (chunk + 1) * G_CHUNK].rearrange(
                             "(t p) k -> p t k", p=P
                         ),
                     )
@@ -188,12 +189,12 @@ def tile_linear_pa_k_kernel(tc, x, weights, path_weights, grad_out, out):
             if s + 1 < len(runs):
                 for i in runs[s + 1]:
                     sort_words(i)
-            for row, scaled in finished:
-                write_out(row, scaled)
-            finished = []
             if s < len(runs):
                 for i in runs[s]:
                     transpose(i)
+            for row, scaled in finished:
+                write_out(row, scaled)
+            finished = []
             if 1 <= s <= len(runs):
                 for i in runs[s - 1]:
                     quantise(i)

@@ -25,11 +25,9 @@ PASSES = K // K_PASS
 NODE_TILES = NODES // P
 BLOCKS = 4
 
-W_PASSES = 4
-W_CHUNK = W_PASSES * K_PASS
-G_PASSES = 2
-G_CHUNK = G_PASSES * K_PASS
-LOAD_AHEAD = 18
+SETS = [[2, 2, 4, 8], [8, 8], [8, 8], [8, 4, 2, 2]]
+PART = 4
+LOAD_AHEAD = 16
 RUN = 2
 
 FLOPS = 2 * NODES * ROWS * K * C_IN
@@ -40,10 +38,10 @@ def tile_linear_pa_k_kernel(tc, x, weights, path_weights, grad_out, out):
     nc = tc.nc
     with ExitStack() as ctx:
         consts = ctx.enter_context(tc.tile_pool(name="consts", bufs=1))
-        w_raw_pool = ctx.enter_context(tc.tile_pool(name="w_raw", bufs=6))
-        g_raw_pool = ctx.enter_context(tc.tile_pool(name="g_raw", bufs=12))
+        raw_pool = ctx.enter_context(tc.tile_pool(name="raw", bufs=8))
         sorted_pool = ctx.enter_context(tc.tile_pool(name="sorted", bufs=4))
-        grouped_pool = ctx.enter_context(tc.tile_pool(name="grouped", bufs=5))
+        w_grouped_pool = ctx.enter_context(tc.tile_pool(name="w_grouped", bufs=2))
+        g_grouped_pool = ctx.enter_context(tc.tile_pool(name="g_grouped", bufs=5))
         g_mx_pool = ctx.enter_context(tc.tile_pool(name="g_mx", bufs=6))
         out_pool = ctx.enter_context(tc.tile_pool(name="out", bufs=2))
         bank_pool = ctx.enter_context(tc.psum_pool(name="bank", bufs=6))
@@ -66,89 +64,130 @@ def tile_linear_pa_k_kernel(tc, x, weights, path_weights, grad_out, out):
             w_codes.append(codes)
             w_scales.append(scales)
 
+        loads = []
         groups = []
+        ready_after = []
+
+        def add_weights(degree, first, passes):
+            loads.append(weights[degree][:, first * K_PASS : (first + passes) * K_PASS].unsqueeze(1))
+            for q in range(passes // BLOCKS):
+                groups.append(("w", len(loads) - 1, q, [(degree, first + q * BLOCKS + b) for b in range(BLOCKS)]))
+                ready_after.append([("w", len(groups) - 1, degree, first + q * BLOCKS)])
+
+        def add_set(row, first, passes):
+            tiles = max(1, BLOCKS // passes)
+            for t in range(0, NODE_TILES, tiles):
+                loads.append(
+                    grad_out[t * P : (t + tiles) * P, row, first * K_PASS : (first + passes) * K_PASS].rearrange(
+                        "(t p) k -> p t k", p=P
+                    )
+                )
+                units = [(row, first, passes, c, t + u) for u in range(tiles) for c in range(passes)]
+                for q in range(len(units) // BLOCKS):
+                    groups.append(("g", len(loads) - 1, q, units[q * BLOCKS : (q + 1) * BLOCKS]))
+                    ready_after.append([])
+            ready_after[-1] = [("g", row, first, c) for c in range(passes)]
+
         for row in range(ROWS):
-            first_of_degree = row == 0 or DEGREE_OF_ROW[row] != DEGREE_OF_ROW[row - 1]
-            for k_pass in range(PASSES):
-                if first_of_degree and k_pass % W_PASSES == 0:
-                    groups.append(("w", DEGREE_OF_ROW[row], k_pass // W_PASSES))
-                groups.append(("g", row, k_pass))
+            first = 0
+            new_degree = row == 0 or DEGREE_OF_ROW[row] != DEGREE_OF_ROW[row - 1]
+            for passes in SETS[row]:
+                if new_degree:
+                    if first % BLOCKS == 0:
+                        add_weights(DEGREE_OF_ROW[row], first, max(passes, BLOCKS))
+                add_set(row, first, passes)
+                first += passes
 
         raw = {}
-        blocks = {}
         sorted_words = {}
-        grouped = {}
+        w_grouped = {}
+        g_grouped = {}
         g_mx = {}
         acc_of_row = {}
 
         def load(i):
-            kind, a, b = groups[i]
-            if kind == "w":
-                w_raw = w_raw_pool.tile([P, W_CHUNK], BF16)
-                nc.sync.dma_start(out=w_raw[:], in_=weights[a][:, b * W_CHUNK : (b + 1) * W_CHUNK])
-                blocks[i] = w_raw[:].bitcast(F32).rearrange("p (b w) -> p b w", b=BLOCKS)
-            else:
-                chunk, c = divmod(b, G_PASSES)
-                if c == 0:
-                    g_raw = g_raw_pool.tile([P, NODE_TILES, G_CHUNK], BF16)
-                    nc.sync.dma_start(
-                        out=g_raw[:],
-                        in_=grad_out[:, a, chunk * G_CHUNK : (chunk + 1) * G_CHUNK].rearrange(
-                            "(t p) k -> p t k", p=P
-                        ),
-                    )
-                    raw[(a, chunk)] = g_raw
-                blocks[i] = raw[(a, chunk)][:].bitcast(F32)[:, :, c * PAIRS : (c + 1) * PAIRS]
+            tiles, k = loads[i].shape[1], loads[i].shape[2]
+            tile = raw_pool.tile([P, tiles, k], BF16, name="raw")
+            nc.sync.dma_start(out=tile[:], in_=loads[i])
+            raw[i] = tile[:].rearrange("p t k -> p (t k)").bitcast(F32)
+
+        def words_of(i):
+            kind, which, q, units = groups[i]
+            size = BLOCKS * PAIRS
+            return raw[which][:, q * size : (q + 1) * size]
 
         def is_sorted(i):
-            return i >= 4 and i < len(groups) - 2 and i % 4 != 3
+            return i % 4 != 3
 
         def sort_words(i):
             if is_sorted(i):
-                tile = sorted_pool.tile([P, BLOCKS, 2, P], F32)
-                nc.vector.tensor_copy(out=tile[:], in_=blocks[i].rearrange("p b (w u) -> p b u w", u=2))
+                tile = sorted_pool.tile([P, BLOCKS, 2, P], F32, name="sorted")
+                nc.vector.tensor_copy(
+                    out=tile[:], in_=words_of(i).rearrange("p (b w u) -> p b u w", b=BLOCKS, u=2)
+                )
                 sorted_words[i] = tile
 
+        def destination(i, half):
+            kind, which, q, units = groups[i]
+            if kind == "w":
+                if half == 0:
+                    w_grouped[i] = w_grouped_pool.tile([P, BLOCKS, P, PACK], BF16, align_bytes=64, name="w_grouped")
+                words = w_grouped[i][:].rearrange("p b r v -> p (b r v)").bitcast(F32)
+                words = words.rearrange("p (b r u) -> p b r u", r=P, u=2)
+                return words[:, 2 * half : 2 * half + 2, :, :]
+            row, first, passes, c, t = units[2 * half]
+            key = (row, first, c // PART)
+            if key not in g_grouped:
+                g_grouped[key] = g_grouped_pool.tile(
+                    [P, min(PART, passes), NODE_TILES, P * PACK], BF16, align_bytes=64, name="g_grouped"
+                )
+            words = g_grouped[key][:].rearrange("p c t v -> p (c t v)").bitcast(F32)
+            words = words.rearrange("p (c t r u) -> p c t r u", t=NODE_TILES, r=P, u=2)
+            c = c % PART
+            if passes > 1:
+                return words[:, c : c + 2, t, :, :]
+            return words[:, c, t : t + 2, :, :]
+
         def transpose(i):
-            grouped[i] = grouped_pool.tile([P, BLOCKS * P * PACK], BF16, align_bytes=64, name="grouped")
-            words = grouped[i][:].bitcast(F32).rearrange("p (b r u) -> p b r u", b=BLOCKS, u=2)
             for half in range(2):
-                bank = bank_pool.tile([P, 2, 2, P], F32, tag="bank")
+                bank = bank_pool.tile([P, 2, 2, P], F32, name="bank")
                 for b in range(2):
                     for u in range(2):
                         block = 2 * half + b
                         if is_sorted(i):
                             in_ = sorted_words[i][:, block, u, :]
                         else:
-                            in_ = blocks[i][:, block, u:PAIRS:2]
+                            in_ = words_of(i)[:, block * PAIRS + u : (block + 1) * PAIRS : 2]
                         nc.tensor.transpose(bank[:, b, u, :], in_, ident[:])
-                nc.scalar.copy(
-                    out=words[:, 2 * half : 2 * half + 2, :, :], in_=bank[:].rearrange("p b u r -> p b r u")
-                )
+                nc.scalar.copy(out=destination(i, half), in_=bank[:].rearrange("p b u r -> p b r u"))
 
-        def quantise(i):
-            kind, a, b = groups[i]
-            if kind == "w":
-                width = BLOCKS * C_IN
-                cols = slice(b * width, (b + 1) * width)
+        def quantise(job):
+            if job[0] == "w":
+                kind, i, degree, first = job
+                cols = slice(first * C_IN, (first + BLOCKS) * C_IN)
                 nc.vector.quantize_mx(
-                    out=w_codes[a][:, cols].bitcast(E4M3X4), scales=w_scales[a][:, cols], in_=grouped[i][:]
+                    out=w_codes[degree][:, cols].bitcast(E4M3X4),
+                    scales=w_scales[degree][:, cols],
+                    in_=w_grouped[i][:].rearrange("p b r v -> p (b r v)"),
                 )
             else:
-                codes = g_mx_pool.tile([P, NODES], U32, align_bytes=64)
-                scales = g_mx_pool.tile([P, NODES], U8, align_bytes=64)
-                nc.vector.quantize_mx(out=codes[:].bitcast(E5M2X4), scales=scales[:], in_=grouped[i][:])
-                g_mx[i] = (codes, scales)
+                kind, row, first, c = job
+                codes = g_mx_pool.tile([P, NODES], U32, align_bytes=64, name="codes")
+                scales = g_mx_pool.tile([P, NODES], U8, align_bytes=64, name="scales")
+                values = g_grouped[(row, first, c // PART)][:, c % PART, :, :]
+                nc.vector.quantize_mx(
+                    out=codes[:].bitcast(E5M2X4), scales=scales[:], in_=values.rearrange("p t v -> p (t v)")
+                )
+                g_mx[job] = (codes, scales)
 
-        def multiply(i):
-            kind, row, k_pass = groups[i]
-            if kind == "w":
-                return
+        def multiply(job):
+            kind, row, first, c = job
+            k_pass = first + c
             if k_pass == 0:
                 acc_of_row[row] = acc_pool.tile([P, NODES], F32, name="acc")
             degree = DEGREE_OF_ROW[row]
             cols = slice(k_pass * C_IN, (k_pass + 1) * C_IN)
-            codes, scales = g_mx[i]
+            codes, scales = g_mx[job]
             nc.tensor.matmul_mx(
                 out=acc_of_row[row][:],
                 lhsT=w_codes[degree][:, cols].bitcast(E4M3X4),
@@ -172,7 +211,7 @@ def tile_linear_pa_k_kernel(tc, x, weights, path_weights, grad_out, out):
             return scaled
 
         def write_out(row, scaled):
-            back = bank_pool.tile([P, NODE_TILES, C_IN], F32, tag="bank")
+            back = bank_pool.tile([P, NODE_TILES, C_IN], F32, name="bank")
             for t in range(NODE_TILES):
                 nc.tensor.transpose(back[:, t, :], scaled[:, t * P : (t + 1) * P], ident[:])
             result = out_pool.tile([P, NODE_TILES, C_IN], F32)
@@ -181,9 +220,18 @@ def tile_linear_pa_k_kernel(tc, x, weights, path_weights, grad_out, out):
 
         runs = [list(range(i, min(i + RUN, len(groups)))) for i in range(0, len(groups), RUN)]
         loaded = 0
+        to_quantise = []
+        to_multiply = []
         finished = []
-        for s in range(len(runs) + 2):
-            while loaded < min(RUN * s + LOAD_AHEAD, len(groups)):
+        s = 0
+        for i in runs[0]:
+            while loaded <= groups[i][1]:
+                load(loaded)
+                loaded += 1
+            sort_words(i)
+        while s < len(runs) or to_quantise or to_multiply:
+            ahead = min(RUN * s + LOAD_AHEAD, len(groups) - 1)
+            while loaded <= groups[ahead][1]:
                 load(loaded)
                 loaded += 1
             if s + 1 < len(runs):
@@ -195,14 +243,19 @@ def tile_linear_pa_k_kernel(tc, x, weights, path_weights, grad_out, out):
             for row, scaled in finished:
                 write_out(row, scaled)
             finished = []
-            if 1 <= s <= len(runs):
-                for i in runs[s - 1]:
-                    quantise(i)
-            if s >= 2:
-                for i in runs[s - 2]:
-                    multiply(i)
-                    kind, row, k_pass = groups[i]
-                    if kind == "g" and k_pass == PASSES - 1:
-                        finished.append((row, scale_row(row)))
+            now = to_quantise[:RUN]
+            to_quantise = to_quantise[RUN:]
+            for job in now:
+                quantise(job)
+            for job in to_multiply:
+                multiply(job)
+                kind, row, first, c = job
+                if first + c == PASSES - 1:
+                    finished.append((row, scale_row(row)))
+            to_multiply = [job for job in now if job[0] == "g"]
+            if s < len(runs):
+                for i in runs[s]:
+                    to_quantise.extend(ready_after[i])
+            s += 1
         for row, scaled in finished:
             write_out(row, scaled)

@@ -39,7 +39,7 @@ def tile_linear_pa_k_kernel(tc, x, weights, path_weights, grad_out, out):
     with ExitStack() as ctx:
         consts = ctx.enter_context(tc.tile_pool(name="consts", bufs=1))
         raw_pool = ctx.enter_context(tc.tile_pool(name="raw", bufs=8))
-        sorted_pool = ctx.enter_context(tc.tile_pool(name="sorted", bufs=4))
+        sorted_pool = ctx.enter_context(tc.tile_pool(name="sorted", bufs=6))
         w_grouped_pool = ctx.enter_context(tc.tile_pool(name="w_grouped", bufs=2))
         g_grouped_pool = ctx.enter_context(tc.tile_pool(name="g_grouped", bufs=5))
         g_mx_pool = ctx.enter_context(tc.tile_pool(name="g_mx", bufs=6))
@@ -116,16 +116,26 @@ def tile_linear_pa_k_kernel(tc, x, weights, path_weights, grad_out, out):
             size = BLOCKS * PAIRS
             return raw[which][:, q * size : (q + 1) * size]
 
-        def is_sorted(i):
-            return i % 4 != 3
+        def is_sorted(unit):
+            k_pass = unit[1] if len(unit) == 2 else unit[1] + unit[3]
+            return k_pass % 4 != 3
 
         def sort_words(i):
-            if is_sorted(i):
-                tile = sorted_pool.tile([P, BLOCKS, 2, P], F32, name="sorted")
-                nc.vector.tensor_copy(
-                    out=tile[:], in_=words_of(i).rearrange("p (b w u) -> p b u w", b=BLOCKS, u=2)
-                )
-                sorted_words[i] = tile
+            units = groups[i][3]
+            b = 0
+            while b < BLOCKS:
+                end = b
+                while end < BLOCKS and is_sorted(units[end]):
+                    end += 1
+                if end > b:
+                    tile = sorted_pool.tile([P, 2, (end - b) * P], F32, name="sorted")
+                    nc.vector.tensor_copy(
+                        out=tile[:].rearrange("p u (j v) -> p u j v", v=8),
+                        in_=words_of(i)[:, b * PAIRS : end * PAIRS].rearrange("p (j u v) -> p u j v", u=2, v=8),
+                    )
+                    for block in range(b, end):
+                        sorted_words[(i, block)] = tile[:, :, (block - b) * P : (block - b + 1) * P]
+                b = max(end, b + 1)
 
         def destination(i, half):
             kind, which, q, units = groups[i]
@@ -154,8 +164,8 @@ def tile_linear_pa_k_kernel(tc, x, weights, path_weights, grad_out, out):
                 for b in range(2):
                     for u in range(2):
                         block = 2 * half + b
-                        if is_sorted(i):
-                            in_ = sorted_words[i][:, block, u, :]
+                        if (i, block) in sorted_words:
+                            in_ = sorted_words[(i, block)][:, u, :]
                         else:
                             in_ = words_of(i)[:, block * PAIRS + u : (block + 1) * PAIRS : 2]
                         nc.tensor.transpose(bank[:, b, u, :], in_, ident[:])

@@ -27,7 +27,7 @@ BLOCKS = 4
 
 SETS = [[2, 2, 4, 8], [8, 8], [8, 8], [8, 4, 2, 2]]
 PART = 4
-LOAD_AHEAD = 16
+RAW_BUFS = 8
 RUN = 2
 
 FLOPS = 2 * NODES * ROWS * K * C_IN
@@ -38,11 +38,11 @@ def tile_linear_pa_k_kernel(tc, x, weights, path_weights, grad_out, out):
     nc = tc.nc
     with ExitStack() as ctx:
         consts = ctx.enter_context(tc.tile_pool(name="consts", bufs=1))
-        raw_pool = ctx.enter_context(tc.tile_pool(name="raw", bufs=8))
+        raw_pool = ctx.enter_context(tc.tile_pool(name="raw", bufs=RAW_BUFS))
         sorted_pool = ctx.enter_context(tc.tile_pool(name="sorted", bufs=6))
         w_grouped_pool = ctx.enter_context(tc.tile_pool(name="w_grouped", bufs=2))
         g_grouped_pool = ctx.enter_context(tc.tile_pool(name="g_grouped", bufs=5))
-        g_mx_pool = ctx.enter_context(tc.tile_pool(name="g_mx", bufs=6))
+        g_mx_pool = ctx.enter_context(tc.tile_pool(name="g_mx", bufs=8))
         out_pool = ctx.enter_context(tc.tile_pool(name="out", bufs=2))
         bank_pool = ctx.enter_context(tc.psum_pool(name="bank", bufs=6))
         acc_pool = ctx.enter_context(tc.psum_pool(name="acc", bufs=2))
@@ -117,8 +117,8 @@ def tile_linear_pa_k_kernel(tc, x, weights, path_weights, grad_out, out):
             return raw[which][:, q * size : (q + 1) * size]
 
         def is_sorted(unit):
-            k_pass = unit[1] if len(unit) == 2 else unit[1] + unit[3]
-            return k_pass % 4 != 3
+            degree, k_pass = unit if len(unit) == 2 else (DEGREE_OF_ROW[unit[0]], unit[1] + unit[3])
+            return degree == 0 or k_pass not in (7, 11, 14, 15)
 
         def sort_words(i):
             units = groups[i][3]
@@ -158,6 +158,11 @@ def tile_linear_pa_k_kernel(tc, x, weights, path_weights, grad_out, out):
                 return words[:, c : c + 2, t, :, :]
             return words[:, c, t : t + 2, :, :]
 
+        def vector_empties(i):
+            return i < 0
+
+        vector_copies = []
+
         def transpose(i):
             for half in range(2):
                 bank = bank_pool.tile([P, 2, 2, P], F32, name="bank")
@@ -169,7 +174,12 @@ def tile_linear_pa_k_kernel(tc, x, weights, path_weights, grad_out, out):
                         else:
                             in_ = words_of(i)[:, block * PAIRS + u : (block + 1) * PAIRS : 2]
                         nc.tensor.transpose(bank[:, b, u, :], in_, ident[:])
-                nc.scalar.copy(out=destination(i, half), in_=bank[:].rearrange("p b u r -> p b r u"))
+                dst = destination(i, half)
+                src = bank[:].rearrange("p b u r -> p b r u")
+                if half == 1 and vector_empties(i):
+                    vector_copies.append((dst, src))
+                else:
+                    nc.scalar.copy(out=dst, in_=src)
 
         def quantise(job):
             if job[0] == "w":
@@ -208,6 +218,32 @@ def tile_linear_pa_k_kernel(tc, x, weights, path_weights, grad_out, out):
                 stop=(k_pass == PASSES - 1),
             )
 
+        def finish(row):
+            degree = DEGREE_OF_ROW[row]
+            half = NODE_TILES // 2
+            scaled = out_pool.tile([P, NODES], F32, name="scaled")
+            result = out_pool.tile([P, NODE_TILES, C_IN], F32, name="result")
+            for h in range(2):
+                nodes = slice(h * half * P, (h + 1) * half * P)
+                nc.vector.tensor_scalar(
+                    out=scaled[:, nodes],
+                    in0=acc_of_row[row][:, nodes],
+                    scalar1=pw[:, degree : degree + 1],
+                    scalar2=None,
+                    op0=mybir.AluOpType.mult,
+                )
+            for h in range(2):
+                back = bank_pool.tile([P, half, C_IN], F32, name="bank")
+                for t in range(half):
+                    cols = slice((h * half + t) * P, (h * half + t + 1) * P)
+                    nc.tensor.transpose(back[:, t, :], scaled[:, cols], ident[:])
+                tiles = slice(h * half, (h + 1) * half)
+                if h == 0:
+                    nc.scalar.copy(out=result[:, tiles, :], in_=back[:])
+                else:
+                    nc.vector.tensor_copy(out=result[:, tiles, :], in_=back[:])
+            nc.sync.dma_start(out=out[:, row, :].rearrange("(t p) c -> p t c", p=P), in_=result[:])
+
         def scale_row(row):
             degree = DEGREE_OF_ROW[row]
             scaled = out_pool.tile([P, NODES], F32)
@@ -229,6 +265,7 @@ def tile_linear_pa_k_kernel(tc, x, weights, path_weights, grad_out, out):
             nc.scalar.dma_start(out=out[:, row, :].rearrange("(t p) c -> p t c", p=P), in_=result[:])
 
         runs = [list(range(i, min(i + RUN, len(groups)))) for i in range(0, len(groups), RUN)]
+        last_group = {groups[i][1]: i for i in range(len(groups))}
         loaded = 0
         to_quantise = []
         to_multiply = []
@@ -240,32 +277,35 @@ def tile_linear_pa_k_kernel(tc, x, weights, path_weights, grad_out, out):
                 loaded += 1
             sort_words(i)
         while s < len(runs) or to_quantise or to_multiply:
-            ahead = min(RUN * s + LOAD_AHEAD, len(groups) - 1)
-            while loaded <= groups[ahead][1]:
+            while loaded < len(loads) and (loaded < RAW_BUFS or last_group[loaded - RAW_BUFS] < RUN * s):
                 load(loaded)
                 loaded += 1
+            for job in to_multiply:
+                multiply(job)
+                kind, row, first, c = job
+                if first + c == PASSES - 1 and row == ROWS - 1:
+                    finish(row)
+                elif first + c == PASSES - 1:
+                    finished.append((row, scale_row(row)))
+            count = 2
+            now = to_quantise[:count]
+            to_quantise = to_quantise[count:]
+            for job in now:
+                quantise(job)
             if s + 1 < len(runs):
                 for i in runs[s + 1]:
                     sort_words(i)
             if s < len(runs):
                 for i in runs[s]:
                     transpose(i)
+            for dst, src in vector_copies:
+                nc.vector.tensor_copy(out=dst, in_=src)
+            vector_copies.clear()
             for row, scaled in finished:
                 write_out(row, scaled)
             finished = []
-            now = to_quantise[:RUN]
-            to_quantise = to_quantise[RUN:]
-            for job in now:
-                quantise(job)
-            for job in to_multiply:
-                multiply(job)
-                kind, row, first, c = job
-                if first + c == PASSES - 1:
-                    finished.append((row, scale_row(row)))
             to_multiply = [job for job in now if job[0] == "g"]
             if s < len(runs):
                 for i in runs[s]:
                     to_quantise.extend(ready_after[i])
             s += 1
-        for row, scaled in finished:
-            write_out(row, scaled)

@@ -25,7 +25,7 @@ PASSES = K // K_PASS
 NODE_TILES = NODES // P
 BLOCKS = 4
 
-SETS = [[2, 2, 4, 8], [8, 8], [8, 8], [8, 4, 2, 2]]
+SETS = [[4, 4, 8], [8, 8], [8, 8], [8, 4, 2, 1, 1]]
 PART = 4
 RAW_BUFS = 8
 RUN = 2
@@ -88,7 +88,9 @@ def tile_linear_pa_k_kernel(tc, x, weights, path_weights, grad_out, out):
                     ready_after.append([])
             ready_after[-1] = [("g", row, first, c) for c in range(passes)]
 
+        first_group = []
         for row in range(ROWS):
+            first_group.append(len(groups))
             first = 0
             new_degree = row == 0 or DEGREE_OF_ROW[row] != DEGREE_OF_ROW[row - 1]
             for passes in SETS[row]:
@@ -158,11 +160,6 @@ def tile_linear_pa_k_kernel(tc, x, weights, path_weights, grad_out, out):
                 return words[:, c : c + 2, t, :, :]
             return words[:, c, t : t + 2, :, :]
 
-        def vector_empties(i):
-            return i < 0
-
-        vector_copies = []
-
         def transpose(i):
             for half in range(2):
                 bank = bank_pool.tile([P, 2, 2, P], F32, name="bank")
@@ -174,12 +171,7 @@ def tile_linear_pa_k_kernel(tc, x, weights, path_weights, grad_out, out):
                         else:
                             in_ = words_of(i)[:, block * PAIRS + u : (block + 1) * PAIRS : 2]
                         nc.tensor.transpose(bank[:, b, u, :], in_, ident[:])
-                dst = destination(i, half)
-                src = bank[:].rearrange("p b u r -> p b r u")
-                if half == 1 and vector_empties(i):
-                    vector_copies.append((dst, src))
-                else:
-                    nc.scalar.copy(out=dst, in_=src)
+                nc.scalar.copy(out=destination(i, half), in_=bank[:].rearrange("p b u r -> p b r u"))
 
         def quantise(job):
             if job[0] == "w":
@@ -265,6 +257,7 @@ def tile_linear_pa_k_kernel(tc, x, weights, path_weights, grad_out, out):
             nc.scalar.dma_start(out=out[:, row, :].rearrange("(t p) c -> p t c", p=P), in_=result[:])
 
         runs = [list(range(i, min(i + RUN, len(groups)))) for i in range(0, len(groups), RUN)]
+        last_row_step = first_group[ROWS - 1] // RUN
         last_group = {groups[i][1]: i for i in range(len(groups))}
         loaded = 0
         to_quantise = []
@@ -287,9 +280,9 @@ def tile_linear_pa_k_kernel(tc, x, weights, path_weights, grad_out, out):
                     finish(row)
                 elif first + c == PASSES - 1:
                     finished.append((row, scale_row(row)))
-            count = 2
-            now = to_quantise[:count]
-            to_quantise = to_quantise[count:]
+            calls = RUN + (1 if s >= last_row_step else 0)
+            now = to_quantise[:calls]
+            to_quantise = to_quantise[calls:]
             for job in now:
                 quantise(job)
             if s + 1 < len(runs):
@@ -298,9 +291,6 @@ def tile_linear_pa_k_kernel(tc, x, weights, path_weights, grad_out, out):
             if s < len(runs):
                 for i in runs[s]:
                     transpose(i)
-            for dst, src in vector_copies:
-                nc.vector.tensor_copy(out=dst, in_=src)
-            vector_copies.clear()
             for row, scaled in finished:
                 write_out(row, scaled)
             finished = []

@@ -25,7 +25,7 @@ PASSES = K // K_PASS
 NODE_TILES = NODES // P
 BLOCKS = 4
 
-SETS = [[4, 4, 8], [8, 8], [8, 8], [8, 4, 2, 1, 1]]
+SETS = [[8, 8], [8, 8], [8, 8], [8, 4, 2, 1, 1]]
 PART = 4
 RAW_BUFS = 8
 RUN = 2
@@ -74,7 +74,11 @@ def tile_linear_pa_k_kernel(tc, x, weights, path_weights, grad_out, out):
                 groups.append(("w", len(loads) - 1, q, [(degree, first + q * BLOCKS + b) for b in range(BLOCKS)]))
                 ready_after.append([("w", len(groups) - 1, degree, first + q * BLOCKS)])
 
+        one_pass_sets = []
+
         def add_set(row, first, passes):
+            if passes == 1:
+                one_pass_sets.append((row, first))
             tiles = max(1, BLOCKS // passes)
             for t in range(0, NODE_TILES, tiles):
                 loads.append(
@@ -110,7 +114,10 @@ def tile_linear_pa_k_kernel(tc, x, weights, path_weights, grad_out, out):
         def load(i):
             tiles, k = loads[i].shape[1], loads[i].shape[2]
             tile = raw_pool.tile([P, tiles, k], BF16, name="raw")
-            nc.sync.dma_start(out=tile[:], in_=loads[i])
+            halves = 2 if tiles == NODE_TILES else 1
+            for h in range(halves):
+                part = slice(h * tiles // halves, (h + 1) * tiles // halves)
+                nc.sync.dma_start(out=tile[:, part, :], in_=loads[i][:, part, :])
             raw[i] = tile[:].rearrange("p t k -> p (t k)").bitcast(F32)
 
         def words_of(i):
@@ -187,9 +194,15 @@ def tile_linear_pa_k_kernel(tc, x, weights, path_weights, grad_out, out):
                 codes = g_mx_pool.tile([P, NODES], U32, align_bytes=64, name="codes")
                 scales = g_mx_pool.tile([P, NODES], U8, align_bytes=64, name="scales")
                 values = g_grouped[(row, first, c // PART)][:, c % PART, :, :]
-                nc.vector.quantize_mx(
-                    out=codes[:].bitcast(E5M2X4), scales=scales[:], in_=values.rearrange("p t v -> p (t v)")
-                )
+                halves = 2 if (row, first) in one_pass_sets else 1
+                tiles = NODE_TILES // halves
+                for h in range(halves):
+                    cols = slice(h * tiles * P, (h + 1) * tiles * P)
+                    nc.vector.quantize_mx(
+                        out=codes[:, cols].bitcast(E5M2X4),
+                        scales=scales[:, cols],
+                        in_=values[:, h * tiles : (h + 1) * tiles, :].rearrange("p t v -> p (t v)"),
+                    )
                 g_mx[job] = (codes, scales)
 
         def multiply(job):
@@ -230,11 +243,13 @@ def tile_linear_pa_k_kernel(tc, x, weights, path_weights, grad_out, out):
                     cols = slice((h * half + t) * P, (h * half + t + 1) * P)
                     nc.tensor.transpose(back[:, t, :], scaled[:, cols], ident[:])
                 tiles = slice(h * half, (h + 1) * half)
+                dst = out[h * half * P : (h + 1) * half * P, row, :].rearrange("(t p) c -> p t c", p=P)
                 if h == 0:
                     nc.scalar.copy(out=result[:, tiles, :], in_=back[:])
+                    nc.scalar.dma_start(out=dst, in_=result[:, tiles, :])
                 else:
                     nc.vector.tensor_copy(out=result[:, tiles, :], in_=back[:])
-            nc.sync.dma_start(out=out[:, row, :].rearrange("(t p) c -> p t c", p=P), in_=result[:])
+                    nc.sync.dma_start(out=dst, in_=result[:, tiles, :])
 
         def scale_row(row):
             degree = DEGREE_OF_ROW[row]

@@ -25,9 +25,10 @@ PASSES = K // K_PASS
 NODE_TILES = NODES // P
 BLOCKS = 4
 
-SETS = [[8, 8], [8, 8], [8, 8], [8, 4, 2, 1, 1]]
+SETS = [[4, 4, 8], [8, 8], [8, 8], [8, 4, 2, 1, 1]]
 PART = 4
 RAW_BUFS = 8
+PW_STEP = 9
 RUN = 2
 
 FLOPS = 2 * NODES * ROWS * K * C_IN
@@ -44,6 +45,7 @@ def tile_linear_pa_k_kernel(tc, x, weights, path_weights, grad_out, out):
         g_grouped_pool = ctx.enter_context(tc.tile_pool(name="g_grouped", bufs=5))
         g_mx_pool = ctx.enter_context(tc.tile_pool(name="g_mx", bufs=8))
         out_pool = ctx.enter_context(tc.tile_pool(name="out", bufs=2))
+        result_pool = ctx.enter_context(tc.tile_pool(name="result", bufs=ROWS))
         bank_pool = ctx.enter_context(tc.psum_pool(name="bank", bufs=6))
         acc_pool = ctx.enter_context(tc.psum_pool(name="acc", bufs=2))
         ctx.enter_context(tc.manual_schedule())
@@ -51,10 +53,16 @@ def tile_linear_pa_k_kernel(tc, x, weights, path_weights, grad_out, out):
         ident = consts.tile([P, P], F32)
         make_identity(nc, ident[:])
 
-        pw_bf16 = consts.tile([P, DEGREES], BF16)
-        nc.scalar.dma_start(out=pw_bf16[:], in_=path_weights.partition_broadcast(P))
+        pw_row = consts.tile([P, DEGREES], BF16)
+        ones = consts.tile([P, P], BF16)
+        nc.gpsimd.memset(pw_row[:], 0.0)
+        nc.gpsimd.memset(ones[:], 1.0)
         pw = consts.tile([P, DEGREES], F32)
-        nc.vector.tensor_copy(out=pw[:], in_=pw_bf16[:])
+
+        def spread_path_weights():
+            bank = bank_pool.tile([P, DEGREES], F32, name="bank")
+            nc.tensor.matmul(bank[:], lhsT=ones[:], rhs=pw_row[:], start=True, stop=True)
+            nc.vector.tensor_copy(out=pw[:], in_=bank[:])
 
         w_codes = []
         w_scales = []
@@ -227,7 +235,7 @@ def tile_linear_pa_k_kernel(tc, x, weights, path_weights, grad_out, out):
             degree = DEGREE_OF_ROW[row]
             half = NODE_TILES // 2
             scaled = out_pool.tile([P, NODES], F32, name="scaled")
-            result = out_pool.tile([P, NODE_TILES, C_IN], F32, name="result")
+            result = result_pool.tile([P, NODE_TILES, C_IN], F32, name="result")
             for h in range(2):
                 nodes = slice(h * half * P, (h + 1) * half * P)
                 nc.vector.tensor_scalar(
@@ -267,9 +275,9 @@ def tile_linear_pa_k_kernel(tc, x, weights, path_weights, grad_out, out):
             back = bank_pool.tile([P, NODE_TILES, C_IN], F32, name="bank")
             for t in range(NODE_TILES):
                 nc.tensor.transpose(back[:, t, :], scaled[:, t * P : (t + 1) * P], ident[:])
-            result = out_pool.tile([P, NODE_TILES, C_IN], F32)
+            result = result_pool.tile([P, NODE_TILES, C_IN], F32, name="result")
             nc.scalar.copy(out=result[:], in_=back[:])
-            nc.scalar.dma_start(out=out[:, row, :].rearrange("(t p) c -> p t c", p=P), in_=result[:])
+            to_store.append((row, result))
 
         runs = [list(range(i, min(i + RUN, len(groups)))) for i in range(0, len(groups), RUN)]
         last_row_step = first_group[ROWS - 1] // RUN
@@ -277,6 +285,7 @@ def tile_linear_pa_k_kernel(tc, x, weights, path_weights, grad_out, out):
         loaded = 0
         to_quantise = []
         to_multiply = []
+        to_store = []
         finished = []
         s = 0
         for i in runs[0]:
@@ -288,6 +297,10 @@ def tile_linear_pa_k_kernel(tc, x, weights, path_weights, grad_out, out):
             while loaded < len(loads) and (loaded < RAW_BUFS or last_group[loaded - RAW_BUFS] < RUN * s):
                 load(loaded)
                 loaded += 1
+            if s == 0:
+                nc.sync.dma_start(out=pw_row[0:1, :], in_=path_weights.unsqueeze(0))
+            if s == PW_STEP:
+                spread_path_weights()
             for job in to_multiply:
                 multiply(job)
                 kind, row, first, c = job
@@ -309,6 +322,9 @@ def tile_linear_pa_k_kernel(tc, x, weights, path_weights, grad_out, out):
             for row, scaled in finished:
                 write_out(row, scaled)
             finished = []
+            if s == len(runs) - 1:
+                for row, result in to_store:
+                    nc.scalar.dma_start(out=out[:, row, :].rearrange("(t p) c -> p t c", p=P), in_=result[:])
             to_multiply = [job for job in now if job[0] == "g"]
             if s < len(runs):
                 for i in runs[s]:

from contextlib import ExitStack

import concourse.mybir as mybir
from concourse.masks import make_identity

BF16 = mybir.dt.bfloat16
F32 = mybir.dt.float32
U32 = mybir.dt.uint32
U8 = mybir.dt.uint8
E4M3X4 = mybir.dt.float8_e4m3fn_x4
E5M2X4 = mybir.dt.float8_e5m2_x4

P = 128
PACK = 4
K_PASS = P * PACK
PAIRS = K_PASS // 2

NODES = 512
ROWS = 4
DEGREE_OF_ROW = [0, 1, 1, 1]
DEGREES = 2
C_IN = 128
K = 8192
PASSES = K // K_PASS
NODE_TILES = NODES // P
BLOCKS = 4

SETS = [[4, 4, 8], [8, 8], [8, 8], [8, 4, 2, 1, 1]]
PART = 4
RAW_BUFS = 8
PW_STEP = 9
RUN = 2

FLOPS = 2 * NODES * ROWS * K * C_IN
BYTES = 2 * (DEGREES * C_IN * K + NODES * ROWS * K + DEGREES) + 4 * NODES * ROWS * C_IN


def tile_linear_pa_k_kernel(tc, x, weights, path_weights, grad_out, out):
    nc = tc.nc
    with ExitStack() as ctx:
        consts = ctx.enter_context(tc.tile_pool(name="consts", bufs=1))
        raw_pool = ctx.enter_context(tc.tile_pool(name="raw", bufs=RAW_BUFS))
        sorted_pool = ctx.enter_context(tc.tile_pool(name="sorted", bufs=6))
        w_grouped_pool = ctx.enter_context(tc.tile_pool(name="w_grouped", bufs=2))
        g_grouped_pool = ctx.enter_context(tc.tile_pool(name="g_grouped", bufs=5))
        g_mx_pool = ctx.enter_context(tc.tile_pool(name="g_mx", bufs=8))
        out_pool = ctx.enter_context(tc.tile_pool(name="out", bufs=2))
        result_pool = ctx.enter_context(tc.tile_pool(name="result", bufs=ROWS))
        bank_pool = ctx.enter_context(tc.psum_pool(name="bank", bufs=6))
        acc_pool = ctx.enter_context(tc.psum_pool(name="acc", bufs=2))
        ctx.enter_context(tc.manual_schedule())

        ident = consts.tile([P, P], F32)
        make_identity(nc, ident[:])

        pw_row = consts.tile([P, DEGREES], BF16)
        ones = consts.tile([P, P], BF16)
        nc.gpsimd.memset(pw_row[:], 0.0)
        nc.gpsimd.memset(ones[:], 1.0)
        pw = consts.tile([P, DEGREES], F32)

        def spread_path_weights():
            bank = bank_pool.tile([P, DEGREES], F32, name="bank")
            nc.tensor.matmul(bank[:], lhsT=ones[:], rhs=pw_row[:], start=True, stop=True)
            nc.vector.tensor_copy(out=pw[:], in_=bank[:])

        w_codes = []
        w_scales = []
        for degree in range(DEGREES):
            codes = consts.tile([P, PASSES * C_IN], U32, align_bytes=64, name="w_codes%d" % degree)
            scales = consts.tile([P, PASSES * C_IN], U8, align_bytes=64, name="w_scales%d" % degree)
            w_codes.append(codes)
            w_scales.append(scales)

        loads = []
        groups = []
        ready_after = []

        def add_weights(degree, first, passes):
            loads.append(weights[degree][:, first * K_PASS : (first + passes) * K_PASS].unsqueeze(1))
            for q in range(passes // BLOCKS):
                groups.append(("w", len(loads) - 1, q, [(degree, first + q * BLOCKS + b) for b in range(BLOCKS)]))
                ready_after.append([("w", len(groups) - 1, degree, first + q * BLOCKS)])

        one_pass_sets = []

        def add_set(row, first, passes):
            if passes == 1:
                one_pass_sets.append((row, first))
            tiles = max(1, BLOCKS // passes)
            for t in range(0, NODE_TILES, tiles):
                loads.append(
                    grad_out[t * P : (t + tiles) * P, row, first * K_PASS : (first + passes) * K_PASS].rearrange(
                        "(t p) k -> p t k", p=P
                    )
                )
                units = [(row, first, passes, c, t + u) for u in range(tiles) for c in range(passes)]
                for q in range(len(units) // BLOCKS):
                    groups.append(("g", len(loads) - 1, q, units[q * BLOCKS : (q + 1) * BLOCKS]))
                    ready_after.append([])
            ready_after[-1] = [("g", row, first, c) for c in range(passes)]

        first_group = []
        for row in range(ROWS):
            first_group.append(len(groups))
            first = 0
            new_degree = row == 0 or DEGREE_OF_ROW[row] != DEGREE_OF_ROW[row - 1]
            for passes in SETS[row]:
                if new_degree:
                    if first % BLOCKS == 0:
                        add_weights(DEGREE_OF_ROW[row], first, max(passes, BLOCKS))
                add_set(row, first, passes)
                first += passes

        raw = {}
        sorted_words = {}
        w_grouped = {}
        g_grouped = {}
        g_mx = {}
        acc_of_row = {}

        def load(i):
            tiles, k = loads[i].shape[1], loads[i].shape[2]
            tile = raw_pool.tile([P, tiles, k], BF16, name="raw")
            halves = 2 if tiles == NODE_TILES else 1
            for h in range(halves):
                part = slice(h * tiles // halves, (h + 1) * tiles // halves)
                nc.sync.dma_start(out=tile[:, part, :], in_=loads[i][:, part, :])
            raw[i] = tile[:].rearrange("p t k -> p (t k)").bitcast(F32)

        def words_of(i):
            kind, which, q, units = groups[i]
            size = BLOCKS * PAIRS
            return raw[which][:, q * size : (q + 1) * size]

        def is_sorted(unit):
            degree, k_pass = unit if len(unit) == 2 else (DEGREE_OF_ROW[unit[0]], unit[1] + unit[3])
            return degree == 0 or k_pass not in (7, 11, 14, 15)

        def sort_words(i):
            units = groups[i][3]
            b = 0
            while b < BLOCKS:
                end = b
                while end < BLOCKS and is_sorted(units[end]):
                    end += 1
                if end > b:
                    tile = sorted_pool.tile([P, 2, (end - b) * P], F32, name="sorted")
                    nc.vector.tensor_copy(
                        out=tile[:].rearrange("p u (j v) -> p u j v", v=8),
                        in_=words_of(i)[:, b * PAIRS : end * PAIRS].rearrange("p (j u v) -> p u j v", u=2, v=8),
                    )
                    for block in range(b, end):
                        sorted_words[(i, block)] = tile[:, :, (block - b) * P : (block - b + 1) * P]
                b = max(end, b + 1)

        def destination(i, half):
            kind, which, q, units = groups[i]
            if kind == "w":
                if half == 0:
                    w_grouped[i] = w_grouped_pool.tile([P, BLOCKS, P, PACK], BF16, align_bytes=64, name="w_grouped")
                words = w_grouped[i][:].rearrange("p b r v -> p (b r v)").bitcast(F32)
                words = words.rearrange("p (b r u) -> p b r u", r=P, u=2)
                return words[:, 2 * half : 2 * half + 2, :, :]
            row, first, passes, c, t = units[2 * half]
            key = (row, first, c // PART)
            if key not in g_grouped:
                g_grouped[key] = g_grouped_pool.tile(
                    [P, min(PART, passes), NODE_TILES, P * PACK], BF16, align_bytes=64, name="g_grouped"
                )
            words = g_grouped[key][:].rearrange("p c t v -> p (c t v)").bitcast(F32)
            words = words.rearrange("p (c t r u) -> p c t r u", t=NODE_TILES, r=P, u=2)
            c = c % PART
            if passes > 1:
                return words[:, c : c + 2, t, :, :]
            return words[:, c, t : t + 2, :, :]

        def transpose(i):
            for half in range(2):
                bank = bank_pool.tile([P, 2, 2, P], F32, name="bank")
                for b in range(2):
                    for u in range(2):
                        block = 2 * half + b
                        if (i, block) in sorted_words:
                            in_ = sorted_words[(i, block)][:, u, :]
                        else:
                            in_ = words_of(i)[:, block * PAIRS + u : (block + 1) * PAIRS : 2]
                        nc.tensor.transpose(bank[:, b, u, :], in_, ident[:])
                nc.scalar.copy(out=destination(i, half), in_=bank[:].rearrange("p b u r -> p b r u"))

        def quantise(job):
            if job[0] == "w":
                kind, i, degree, first = job
                cols = slice(first * C_IN, (first + BLOCKS) * C_IN)
                nc.vector.quantize_mx(
                    out=w_codes[degree][:, cols].bitcast(E4M3X4),
                    scales=w_scales[degree][:, cols],
                    in_=w_grouped[i][:].rearrange("p b r v -> p (b r v)"),
                )
            else:
                kind, row, first, c = job
                codes = g_mx_pool.tile([P, NODES], U32, align_bytes=64, name="codes")
                scales = g_mx_pool.tile([P, NODES], U8, align_bytes=64, name="scales")
                values = g_grouped[(row, first, c // PART)][:, c % PART, :, :]
                halves = 2 if (row, first) in one_pass_sets else 1
                tiles = NODE_TILES // halves
                for h in range(halves):
                    cols = slice(h * tiles * P, (h + 1) * tiles * P)
                    nc.vector.quantize_mx(
                        out=codes[:, cols].bitcast(E5M2X4),
                        scales=scales[:, cols],
                        in_=values[:, h * tiles : (h + 1) * tiles, :].rearrange("p t v -> p (t v)"),
                    )
                g_mx[job] = (codes, scales)

        def multiply(job):
            kind, row, first, c = job
            k_pass = first + c
            if k_pass == 0:
                acc_of_row[row] = acc_pool.tile([P, NODES], F32, name="acc")
            degree = DEGREE_OF_ROW[row]
            cols = slice(k_pass * C_IN, (k_pass + 1) * C_IN)
            codes, scales = g_mx[job]
            nc.tensor.matmul_mx(
                out=acc_of_row[row][:],
                lhsT=w_codes[degree][:, cols].bitcast(E4M3X4),
                lhsT_scale=w_scales[degree][:, cols],
                rhs=codes[:].bitcast(E5M2X4),
                rhs_scale=scales[:],
                start=(k_pass == 0),
                stop=(k_pass == PASSES - 1),
            )

        def finish(row):
            degree = DEGREE_OF_ROW[row]
            half = NODE_TILES // 2
            scaled = out_pool.tile([P, NODES], F32, name="scaled")
            result = result_pool.tile([P, NODE_TILES, C_IN], F32, name="result")
            for h in range(2):
                nodes = slice(h * half * P, (h + 1) * half * P)
                nc.vector.tensor_scalar(
                    out=scaled[:, nodes],
                    in0=acc_of_row[row][:, nodes],
                    scalar1=pw[:, degree : degree + 1],
                    scalar2=None,
                    op0=mybir.AluOpType.mult,
                )
            for h in range(2):
                back = bank_pool.tile([P, half, C_IN], F32, name="bank")
                for t in range(half):
                    cols = slice((h * half + t) * P, (h * half + t + 1) * P)
                    nc.tensor.transpose(back[:, t, :], scaled[:, cols], ident[:])
                tiles = slice(h * half, (h + 1) * half)
                dst = out[h * half * P : (h + 1) * half * P, row, :].rearrange("(t p) c -> p t c", p=P)
                if h == 0:
                    nc.scalar.copy(out=result[:, tiles, :], in_=back[:])
                    nc.scalar.dma_start(out=dst, in_=result[:, tiles, :])
                else:
                    nc.vector.tensor_copy(out=result[:, tiles, :], in_=back[:])
                    nc.sync.dma_start(out=dst, in_=result[:, tiles, :])

        def scale_row(row):
            degree = DEGREE_OF_ROW[row]
            scaled = out_pool.tile([P, NODES], F32)
            nc.vector.tensor_scalar(
                out=scaled[:],
                in0=acc_of_row[row][:],
                scalar1=pw[:, degree : degree + 1],
                scalar2=None,
                op0=mybir.AluOpType.mult,
            )
            return scaled

        def write_out(row, scaled):
            back = bank_pool.tile([P, NODE_TILES, C_IN], F32, name="bank")
            for t in range(NODE_TILES):
                nc.tensor.transpose(back[:, t, :], scaled[:, t * P : (t + 1) * P], ident[:])
            result = result_pool.tile([P, NODE_TILES, C_IN], F32, name="result")
            nc.scalar.copy(out=result[:], in_=back[:])
            to_store.append((row, result))

        runs = [list(range(i, min(i + RUN, len(groups)))) for i in range(0, len(groups), RUN)]
        last_row_step = first_group[ROWS - 1] // RUN
        last_group = {groups[i][1]: i for i in range(len(groups))}
        loaded = 0
        to_quantise = []
        to_multiply = []
        to_store = []
        finished = []
        s = 0
        for i in runs[0]:
            while loaded <= groups[i][1]:
                load(loaded)
                loaded += 1
            sort_words(i)
        while s < len(runs) or to_quantise or to_multiply:
            while loaded < len(loads) and (loaded < RAW_BUFS or last_group[loaded - RAW_BUFS] < RUN * s):
                load(loaded)
                loaded += 1
            if s == 0:
                nc.sync.dma_start(out=pw_row[0:1, :], in_=path_weights.unsqueeze(0))
            if s == PW_STEP:
                spread_path_weights()
            for job in to_multiply:
                multiply(job)
                kind, row, first, c = job
                if first + c == PASSES - 1 and row == ROWS - 1:
                    finish(row)
                elif first + c == PASSES - 1:
                    finished.append((row, scale_row(row)))
            calls = RUN + (1 if s >= last_row_step else 0)
            now = to_quantise[:calls]
            to_quantise = to_quantise[calls:]
            for job in now:
                quantise(job)
            if s + 1 < len(runs):
                for i in runs[s + 1]:
                    sort_words(i)
            if s < len(runs):
                for i in runs[s]:
                    transpose(i)
            for row, scaled in finished:
                write_out(row, scaled)
            finished = []
            if s == len(runs) - 1:
                for row, result in to_store:
                    nc.scalar.dma_start(out=out[:, row, :].rearrange("(t p) c -> p t c", p=P), in_=result[:])
            to_multiply = [job for job in now if job[0] == "g"]
            if s < len(runs):
                for i in runs[s]:
                    to_quantise.extend(ready_after[i])
            s += 1
